import numpy as np
import ml_dtypes


def mxq(x, axis, fmt="e4m3"):
    dtype, down = {"e4m3": (ml_dtypes.float8_e4m3fn, 7), "e5m2": (ml_dtypes.float8_e5m2, 14)}[fmt]
    v = np.moveaxis(np.asarray(x, np.float32).astype(ml_dtypes.bfloat16).astype(np.float64), axis, -1)
    blocks = v.reshape(v.shape[:-1] + (-1, 32))
    amax = np.abs(blocks).max(-1, keepdims=True)
    byte = np.maximum(np.where(amax > 0, np.frexp(amax)[1] - 1 + 127, 0) - down, 1)
    scale = np.exp2(byte - 127.0)
    codes = (blocks / scale).astype(np.float32).astype(dtype).astype(np.float64)
    return np.moveaxis((codes * scale).reshape(v.shape), -1, axis)


WIDE = False


def mx_kscale(k):
    if not WIDE:
        return np.ones(k)
    levels = np.array([10, -10, 5, -5, 0])
    a = np.random.permutation(np.resize(levels, k // 512 * 4)).reshape(k // 512, 4)
    idx = np.arange(k)
    return np.exp2(a[idx // 512, idx % 128 // 32])


BF16 = ml_dtypes.bfloat16


def bf(x):
    return np.asarray(x, np.float32).astype(BF16)


def f64(x):
    return np.asarray(x).astype(np.float64)


B, EMBED, HIDDEN, C, E = 4096, 768, 1024, 3, 512
LS = 0.1


def setup_inputs():
    s, t = mx_kscale(HIDDEN), mx_kscale(E)
    x = np.random.standard_normal((B, HIDDEN))
    r = 0.6 + 0.8 * np.random.random((C, 1, 1))
    return {"h": bf(x / (1.0 + np.exp(-1.702 * x)) * s),
            "W3": bf(np.random.standard_normal((HIDDEN, E)) * 1.5 / np.sqrt(HIDDEN) / s[:, None] * t),
            "b3": bf(np.random.standard_normal(E) * 0.5 * t),
            "class_weight": bf(np.random.standard_normal((C, E, E)) * r * 0.14 / E / t[:, None]),
            "centroids": bf(np.random.standard_normal((C, E)) * 0.14 / np.sqrt(E))}


def reference(h, W3, b3, class_weight, centroids):
    z = (mxq(f64(h), 1, "e4m3") @ mxq(f64(W3), 0, "e4m3")) + f64(b3)
    weighted = (mxq(z, 1, "e4m3") @ mxq(f64(class_weight), 1, "e4m3")).transpose(1, 0, 2)
    diff = weighted - f64(centroids)[None, :, :]
    dist_sq = np.sum(diff * diff, axis=-1)
    log_kernel = -dist_sq / (2.0 * LS * LS)
    kernel_vals = np.exp(log_kernel)
    e = np.exp(log_kernel - log_kernel.max(-1, keepdims=True))
    probs = e / e.sum(-1, keepdims=True)
    uncertainty = 1.0 - kernel_vals.max(-1)
    return probs, probs[None], kernel_vals, uncertainty

@@ -1,0 +1,202 @@
+from contextlib import ExitStack
+
+import concourse.bass as bass
+import concourse.mybir as mybir
+import concourse.tile as tile
+from concourse.masks import make_identity
+
+F32 = mybir.dt.float32
+BF16 = mybir.dt.bfloat16
+U32 = mybir.dt.uint32
+U8 = mybir.dt.uint8
+FP8X4 = mybir.dt.float8_e4m3fn_x4
+ALU = mybir.AluOpType
+ACT = mybir.ActivationFunctionType
+AX = mybir.AxisListType
+
+P = 128
+B, HIDDEN, E, C = 4096, 1024, 512, 3
+LS = 0.1
+J = B // P
+UNIT = 2
+N_UNITS = J // UNIT
+FLOPS = 2 * B * HIDDEN * E + 2 * B * E * C * E
+
+
+def tile_duqhead_pa_t_kernel(tc, h, W3, b3, class_weight, centroids, out_0, out_1, out_2, out_3):
+    nc = tc.nc
+    with ExitStack() as ctx:
+        const = ctx.enter_context(tc.tile_pool(name="const", bufs=1))
+        hpool = ctx.enter_context(tc.tile_pool(name="hpool", bufs=6))
+        stage = ctx.enter_context(tc.tile_pool(name="stage", bufs=3))
+        dpool = ctx.enter_context(tc.tile_pool(name="dpool", bufs=6))
+        psum_t = ctx.enter_context(tc.psum_pool(name="psum_t", bufs=2))
+        psum_z = ctx.enter_context(tc.psum_pool(name="psum_z", bufs=2))
+        psum_w = ctx.enter_context(tc.psum_pool(name="psum_w", bufs=4))
+
+        h_view = h.rearrange("(p j) k -> p j k", j=J)
+        w3raw = const.tile([P, 4, 2 * E], BF16)
+        nc.sync.dma_start(out=w3raw[:], in_=W3.rearrange("(a q e) c -> q a (e c)", a=4, q=P, e=2))
+        h_tiles = []
+
+        def load_h(u):
+            h_sb = hpool.tile([P, UNIT, HIDDEN], BF16, name="h_sb")
+            nc.sync.dma_start(out=h_sb[:], in_=h_view[:, u * UNIT:(u + 1) * UNIT, :])
+            h_tiles.append(h_sb)
+
+        load_h(0)
+        bias_bf = const.tile([P, 4], BF16)
+        nc.sync.dma_start(out=bias_bf[:], in_=b3.rearrange("(m t) -> m t", t=4))
+        cent_bc = const.tile([P, C * E], BF16)
+        nc.sync.dma_start(out=cent_bc[:], in_=centroids.rearrange("c d -> (c d)").partition_broadcast(P))
+        cwraw = const.tile([P, C, 4, E], BF16)
+        cw_view = class_weight.rearrange("c (p j) d -> p c j d", j=4)
+        nc.sync.dma_start(out=cwraw[:, 0], in_=cw_view[:, 0])
+        load_h(1)
+        nc.sync.dma_start(out=cwraw[:, 1], in_=cw_view[:, 1])
+        nc.sync.dma_start(out=cwraw[:, 2], in_=cw_view[:, 2])
+
+        ident = const.tile([P, P], F32)
+        make_identity(nc, ident[:])
+        warm = const.tile([P, 1], F32)
+        nc.vector.memset(warm[:], 0.0)
+        warm2 = const.tile([P, 1], F32)
+        nc.scalar.activation(out=warm2[:], in_=warm[:], func=ACT.Exp)
+
+        w3grp = const.tile([P, 2, E, 4], BF16, align_bytes=64)
+        w3codes = const.tile([P, 2, E], U32, align_bytes=64)
+        w3scales = const.tile([P, 2, E], U8, align_bytes=64)
+
+        def w3_regroup(eng_copy, g, t0, t1):
+            src = w3raw[:, 2 * g:2 * g + 2, :].rearrange("q u (e m t) -> q t m (u e)", e=2, t=4)
+            dst = w3grp[:, g].rearrange("q (t m) x -> q t m x", t=4)
+            eng_copy(out=dst[:, t0:t1], in_=src[:, t0:t1])
+
+        w3_regroup(nc.vector.tensor_copy, 0, 0, 4)
+        w3_regroup(nc.scalar.copy, 1, 2, 4)
+        w3_regroup(nc.vector.tensor_copy, 1, 0, 2)
+        for g in range(2):
+            nc.vector.quantize_mx(
+                out=w3codes[:, g, :].bitcast(FP8X4),
+                scales=w3scales[:, g, :],
+                in_=w3grp[:, g].rearrange("q c x -> q (c x)"),
+            )
+        bias_f = const.tile([P, 4], F32)
+        nc.vector.tensor_copy(out=bias_f[:], in_=bias_bf[:])
+
+        cwgrp = const.tile([P, C, E, 4], BF16, align_bytes=64)
+        cwcodes = const.tile([P, C, E], U32, align_bytes=64)
+        cwscales = const.tile([P, C, E], U8, align_bytes=64)
+
+        def cw_prepare(eng_copy, c):
+            eng_copy(
+                out=cwgrp[:, c].rearrange("p (a i) j -> p a j i", i=4),
+                in_=cwraw[:, c].rearrange("p j (a i) -> p a j i", i=4),
+            )
+
+        def cw_quantise(c):
+            nc.vector.quantize_mx(
+                out=cwcodes[:, c, :].bitcast(FP8X4),
+                scales=cwscales[:, c, :],
+                in_=cwgrp[:, c].rearrange("p d j -> p (d j)"),
+            )
+
+        dist = const.tile([P, J, C], F32)
+
+        for u in range(N_UNITS):
+            if u + 2 < N_UNITS:
+                load_h(u + 2)
+            h_words = h_tiles[u][:].bitcast(F32)
+            hgrp = stage.tile([P, 2, UNIT * P, 4], BF16, align_bytes=64)
+            hgrp_words = hgrp[:].bitcast(F32)
+            for jl in range(UNIT):
+                xt = psum_t.tile([P, 4, P], F32)
+                for a in range(4):
+                    nc.tensor.transpose(xt[:, a, :], h_words[:, jl, a * P:(a + 1) * P], ident[:])
+                nc.scalar.copy(
+                    out=hgrp_words[:, :, jl * P:(jl + 1) * P, :],
+                    in_=xt[:].rearrange("q (g u) w -> q g w u", g=2),
+                )
+            hcodes = stage.tile([P, 2, UNIT * P], U32, align_bytes=64)
+            hscales = stage.tile([P, 2, UNIT * P], U8, align_bytes=64)
+            nc.vector.quantize_mx(
+                out=hcodes[:].rearrange("q g w -> q (g w)").bitcast(FP8X4),
+                scales=hscales[:].rearrange("q g w -> q (g w)"),
+                in_=hgrp[:].rearrange("q g w x -> q (g w x)"),
+            )
+            if u == 0:
+                cw_prepare(nc.vector.tensor_copy, 0)
+                cw_prepare(nc.scalar.copy, 1)
+                cw_prepare(nc.vector.tensor_copy, 2)
+                for c in range(C):
+                    cw_quantise(c)
+
+            zgrp = stage.tile([P, UNIT * P, 4], BF16, align_bytes=64)
+            for jl in range(UNIT):
+                cols = slice(jl * P, (jl + 1) * P)
+                z_ps = psum_z.tile([P, 4, P], F32)
+                for t in range(4):
+                    for g in range(2):
+                        nc.tensor.matmul_mx(
+                            out=z_ps[:, t, :],
+                            lhsT=w3codes[:, g, t * P:(t + 1) * P].bitcast(FP8X4),
+                            lhsT_scale=w3scales[:, g, t * P:(t + 1) * P],
+                            rhs=hcodes[:, g, cols].bitcast(FP8X4),
+                            rhs_scale=hscales[:, g, cols],
+                            start=(g == 0),
+                            stop=(g == 1),
+                        )
+                nc.vector.tensor_tensor(
+                    out=zgrp[:, cols, :],
+                    in0=z_ps[:].rearrange("m t b -> m b t"),
+                    in1=bias_f[:].unsqueeze(1).to_broadcast([P, P, 4]),
+                    op=ALU.add,
+                )
+            zcodes = stage.tile([P, UNIT * P], U32, align_bytes=64)
+            zscales = stage.tile([P, UNIT * P], U8, align_bytes=64)
+            nc.vector.quantize_mx(
+                out=zcodes[:].bitcast(FP8X4),
+                scales=zscales[:],
+                in_=zgrp[:].rearrange("m b t -> m (b t)"),
+            )
+            for jl in range(UNIT):
+                cols = slice(jl * P, (jl + 1) * P)
+                j = u * UNIT + jl
+                for c in range(C):
+                    w_ps = psum_w.tile([P, E], F32)
+                    nc.tensor.matmul_mx(
+                        out=w_ps[:],
+                        lhsT=zcodes[:, cols].bitcast(FP8X4),
+                        lhsT_scale=zscales[:, cols],
+                        rhs=cwcodes[:, c, :].bitcast(FP8X4),
+                        rhs_scale=cwscales[:, c, :],
+                        start=True,
+                        stop=True,
+                    )
+                    diff = dpool.tile([P, E], F32)
+                    nc.vector.tensor_tensor(out=diff[:], in0=w_ps[:], in1=cent_bc[:, c * E:(c + 1) * E], op=ALU.subtract)
+                    nc.scalar.activation(out=diff[:], in_=diff[:], func=ACT.Square, accum_out=dist[:, j, c:c + 1])
+
+        neg = -1.0 / (2.0 * LS * LS)
+        kv = const.tile([P, J, C], F32)
+        nc.scalar.activation(out=kv[:], in_=dist[:], func=ACT.Exp, scale=neg)
+        nc.sync.dma_start(out=out_2.rearrange("(p j) c -> p j c", j=J), in_=kv[:])
+        dmin = const.tile([P, J], F32)
+        nc.vector.tensor_reduce(out=dmin[:], in_=dist[:], axis=AX.X, op=ALU.min)
+        shifted = const.tile([P, J, C], F32)
+        nc.vector.tensor_tensor(out=shifted[:], in0=dist[:], in1=dmin[:].unsqueeze(2).to_broadcast([P, J, C]), op=ALU.subtract)
+        ex = const.tile([P, J, C], F32)
+        nc.scalar.activation(out=ex[:], in_=shifted[:], func=ACT.Exp, scale=neg)
+        ssum = const.tile([P, J], F32)
+        nc.vector.tensor_reduce(out=ssum[:], in_=ex[:], axis=AX.X, op=ALU.add)
+        rsum = const.tile([P, J], F32)
+        nc.vector.reciprocal(out=rsum[:], in_=ssum[:])
+        probs = const.tile([P, J, C], F32)
+        nc.vector.tensor_tensor(out=probs[:], in0=ex[:], in1=rsum[:].unsqueeze(2).to_broadcast([P, J, C]), op=ALU.mult)
+        nc.sync.dma_start(out=out_0.rearrange("(p j) c -> p j c", j=J), in_=probs[:])
+        nc.scalar.dma_start(out=out_1.rearrange("o (p j) c -> (o p) j c", j=J), in_=probs[:])
+        kmax = const.tile([P, J], F32)
+        nc.vector.tensor_reduce(out=kmax[:], in_=kv[:], axis=AX.X, op=ALU.max)
+        unc = const.tile([P, J], F32)
+        nc.vector.tensor_scalar(out=unc[:], in0=kmax[:], scalar1=-1.0, scalar2=1.0, op0=ALU.mult, op1=ALU.add)
+        nc.scalar.dma_start(out=out_3.rearrange("(p j) -> p j", j=J), in_=unc[:])

@@ -1,8 +1,6 @@
 from contextlib import ExitStack
 
-import concourse.bass as bass
 import concourse.mybir as mybir
-import concourse.tile as tile
 from concourse.masks import make_identity
 
 F32 = mybir.dt.float32
@@ -19,42 +17,48 @@ B, HIDDEN, E, C = 4096, 1024, 512, 3
 LS = 0.1
 J = B // P
 UNIT = 2
+UW = UNIT * P
 N_UNITS = J // UNIT
+CD = 2
 FLOPS = 2 * B * HIDDEN * E + 2 * B * E * C * E
 
 
 def tile_duqhead_pa_t_kernel(tc, h, W3, b3, class_weight, centroids, out_0, out_1, out_2, out_3):
     nc = tc.nc
     with ExitStack() as ctx:
+        ctx.enter_context(tc.manual_schedule())
         const = ctx.enter_context(tc.tile_pool(name="const", bufs=1))
-        hpool = ctx.enter_context(tc.tile_pool(name="hpool", bufs=6))
-        stage = ctx.enter_context(tc.tile_pool(name="stage", bufs=3))
+        hpool = ctx.enter_context(tc.tile_pool(name="hpool", bufs=5))
+        stage = ctx.enter_context(tc.tile_pool(name="stage", bufs=2))
         dpool = ctx.enter_context(tc.tile_pool(name="dpool", bufs=6))
-        psum_t = ctx.enter_context(tc.psum_pool(name="psum_t", bufs=2))
-        psum_z = ctx.enter_context(tc.psum_pool(name="psum_z", bufs=2))
-        psum_w = ctx.enter_context(tc.psum_pool(name="psum_w", bufs=4))
+        sqpool = ctx.enter_context(tc.tile_pool(name="sqpool", bufs=3))
+        psum = ctx.enter_context(tc.psum_pool(name="psum", bufs=1))
+
+        crow = const.tile([P, P], BF16)
+        nc.vector.memset(crow[:], 0.0)
+        nc.scalar.dma_start(out=crow[0:4 * C, :], in_=centroids.rearrange("c (k p) -> (c k) p", p=P))
+        bias_bf = const.tile([P, 4], BF16)
+        nc.scalar.dma_start(out=bias_bf[:], in_=b3.rearrange("(m t) -> m t", t=4))
 
         h_view = h.rearrange("(p j) k -> p j k", j=J)
-        w3raw = const.tile([P, 4, 2 * E], BF16)
-        nc.sync.dma_start(out=w3raw[:], in_=W3.rearrange("(a q e) c -> q a (e c)", a=4, q=P, e=2))
-        h_tiles = []
+        h_sb = {}
 
         def load_h(u):
-            h_sb = hpool.tile([P, UNIT, HIDDEN], BF16, name="h_sb")
-            nc.sync.dma_start(out=h_sb[:], in_=h_view[:, u * UNIT:(u + 1) * UNIT, :])
-            h_tiles.append(h_sb)
+            h_sb[u] = hpool.tile([P, UNIT, HIDDEN], BF16, name="h_sb")
+            nc.sync.dma_start(out=h_sb[u][:], in_=h_view[:, u * UNIT:(u + 1) * UNIT, :])
 
         load_h(0)
-        bias_bf = const.tile([P, 4], BF16)
-        nc.sync.dma_start(out=bias_bf[:], in_=b3.rearrange("(m t) -> m t", t=4))
-        cent_bc = const.tile([P, C * E], BF16)
-        nc.sync.dma_start(out=cent_bc[:], in_=centroids.rearrange("c d -> (c d)").partition_broadcast(P))
+        w3raw = const.tile([P, 4, 2 * E], BF16)
+        w3_view = W3.rearrange("(a q e) c -> q a (e c)", a=4, q=P, e=2)
+        nc.sync.dma_start(out=w3raw[:, 0:2], in_=w3_view[:, 0:2])
+        nc.sync.dma_start(out=w3raw[:, 2:4], in_=w3_view[:, 2:4])
+        load_h(1)
         cwraw = const.tile([P, C, 4, E], BF16)
         cw_view = class_weight.rearrange("c (p j) d -> p c j d", j=4)
-        nc.sync.dma_start(out=cwraw[:, 0], in_=cw_view[:, 0])
-        load_h(1)
-        nc.sync.dma_start(out=cwraw[:, 1], in_=cw_view[:, 1])
-        nc.sync.dma_start(out=cwraw[:, 2], in_=cw_view[:, 2])
+        for c in range(C):
+            nc.sync.dma_start(out=cwraw[:, c], in_=cw_view[:, c])
+        load_h(2)
+        load_h(3)
 
         ident = const.tile([P, P], F32)
         make_identity(nc, ident[:])
@@ -62,6 +66,11 @@ def tile_duqhead_pa_t_kernel(tc, h, W3, b3, class_weight, centroids, out_0, out_
         nc.vector.memset(warm[:], 0.0)
         warm2 = const.tile([P, 1], F32)
         nc.scalar.activation(out=warm2[:], in_=warm[:], func=ACT.Exp)
+        ones = const.tile([P, 1], F32)
+        nc.vector.memset(ones[:], 1.0)
+        ident_bf = const.tile([P, 4 * C], BF16)
+        nc.vector.tensor_copy(out=ident_bf[:], in_=ident[:, 0:4 * C])
+
 
         w3grp = const.tile([P, 2, E, 4], BF16, align_bytes=64)
         w3codes = const.tile([P, 2, E], U32, align_bytes=64)
@@ -72,26 +81,21 @@ def tile_duqhead_pa_t_kernel(tc, h, W3, b3, class_weight, centroids, out_0, out_
             dst = w3grp[:, g].rearrange("q (t m) x -> q t m x", t=4)
             eng_copy(out=dst[:, t0:t1], in_=src[:, t0:t1])
 
-        w3_regroup(nc.vector.tensor_copy, 0, 0, 4)
-        w3_regroup(nc.scalar.copy, 1, 2, 4)
-        w3_regroup(nc.vector.tensor_copy, 1, 0, 2)
-        for g in range(2):
+        def w3_quantise(g):
             nc.vector.quantize_mx(
                 out=w3codes[:, g, :].bitcast(FP8X4),
                 scales=w3scales[:, g, :],
                 in_=w3grp[:, g].rearrange("q c x -> q (c x)"),
             )
-        bias_f = const.tile([P, 4], F32)
-        nc.vector.tensor_copy(out=bias_f[:], in_=bias_bf[:])
 
         cwgrp = const.tile([P, C, E, 4], BF16, align_bytes=64)
         cwcodes = const.tile([P, C, E], U32, align_bytes=64)
         cwscales = const.tile([P, C, E], U8, align_bytes=64)
 
-        def cw_prepare(eng_copy, c):
+        def cw_regroup(eng_copy, c, d0, d1):
             eng_copy(
-                out=cwgrp[:, c].rearrange("p (a i) j -> p a j i", i=4),
-                in_=cwraw[:, c].rearrange("p j (a i) -> p a j i", i=4),
+                out=cwgrp[:, c, d0:d1, :].rearrange("p (a i) j -> p a j i", i=4),
+                in_=cwraw[:, c, :, d0:d1].rearrange("p j (a i) -> p a j i", i=4),
             )
 
         def cw_quantise(c):
@@ -101,92 +105,249 @@ def tile_duqhead_pa_t_kernel(tc, h, W3, b3, class_weight, centroids, out_0, out_
                 in_=cwgrp[:, c].rearrange("p d j -> p (d j)"),
             )
 
-        dist = const.tile([P, J, C], F32)
+        dist = const.tile([P, C, J], F32)
+        dist_ps = psum.tile([P, J], F32)
 
-        for u in range(N_UNITS):
-            if u + 2 < N_UNITS:
-                load_h(u + 2)
-            h_words = h_tiles[u][:].bitcast(F32)
-            hgrp = stage.tile([P, 2, UNIT * P, 4], BF16, align_bytes=64)
-            hgrp_words = hgrp[:].bitcast(F32)
+        xt, hgrp, hcodes, hscales = {}, {}, {}, {}
+        z_ps, zgrp, zcodes, zscales = {}, {}, {}, {}
+        w_ps, diff, wd_ps, sq = {}, {}, {}, {}
+
+        def transposes(u):
+            words = h_sb[u][:].bitcast(F32)
             for jl in range(UNIT):
-                xt = psum_t.tile([P, 4, P], F32)
+                xt[u, jl] = psum.tile([P, 4, P], F32, name="xt%d" % jl)
                 for a in range(4):
-                    nc.tensor.transpose(xt[:, a, :], h_words[:, jl, a * P:(a + 1) * P], ident[:])
-                nc.scalar.copy(
-                    out=hgrp_words[:, :, jl * P:(jl + 1) * P, :],
-                    in_=xt[:].rearrange("q (g u) w -> q g w u", g=2),
-                )
-            hcodes = stage.tile([P, 2, UNIT * P], U32, align_bytes=64)
-            hscales = stage.tile([P, 2, UNIT * P], U8, align_bytes=64)
-            nc.vector.quantize_mx(
-                out=hcodes[:].rearrange("q g w -> q (g w)").bitcast(FP8X4),
-                scales=hscales[:].rearrange("q g w -> q (g w)"),
-                in_=hgrp[:].rearrange("q g w x -> q (g w x)"),
-            )
-            if u == 0:
-                cw_prepare(nc.vector.tensor_copy, 0)
-                cw_prepare(nc.scalar.copy, 1)
-                cw_prepare(nc.vector.tensor_copy, 2)
-                for c in range(C):
-                    cw_quantise(c)
+                    nc.tensor.transpose(xt[u, jl][:, a, :], words[:, jl, a * P:(a + 1) * P], ident[:])
 
-            zgrp = stage.tile([P, UNIT * P, 4], BF16, align_bytes=64)
-            for jl in range(UNIT):
-                cols = slice(jl * P, (jl + 1) * P)
-                z_ps = psum_z.tile([P, 4, P], F32)
-                for t in range(4):
-                    for g in range(2):
-                        nc.tensor.matmul_mx(
-                            out=z_ps[:, t, :],
-                            lhsT=w3codes[:, g, t * P:(t + 1) * P].bitcast(FP8X4),
-                            lhsT_scale=w3scales[:, g, t * P:(t + 1) * P],
-                            rhs=hcodes[:, g, cols].bitcast(FP8X4),
-                            rhs_scale=hscales[:, g, cols],
-                            start=(g == 0),
-                            stop=(g == 1),
-                        )
-                nc.vector.tensor_tensor(
-                    out=zgrp[:, cols, :],
-                    in0=z_ps[:].rearrange("m t b -> m b t"),
-                    in1=bias_f[:].unsqueeze(1).to_broadcast([P, P, 4]),
-                    op=ALU.add,
-                )
-            zcodes = stage.tile([P, UNIT * P], U32, align_bytes=64)
-            zscales = stage.tile([P, UNIT * P], U8, align_bytes=64)
-            nc.vector.quantize_mx(
-                out=zcodes[:].bitcast(FP8X4),
-                scales=zscales[:],
-                in_=zgrp[:].rearrange("m b t -> m (b t)"),
+        def h_out(u, jl, eng_copy):
+            if jl == 0:
+                hgrp[u] = stage.tile([P, 2, UW, 4], BF16, align_bytes=64, name="hgrp")
+            eng_copy(
+                out=hgrp[u][:].bitcast(F32)[:, :, jl * P:(jl + 1) * P, :],
+                in_=xt[u, jl][:].rearrange("q (g u) w -> q g w u", g=2),
             )
-            for jl in range(UNIT):
-                cols = slice(jl * P, (jl + 1) * P)
-                j = u * UNIT + jl
-                for c in range(C):
-                    w_ps = psum_w.tile([P, E], F32)
+
+        def h_quantise(u):
+            hcodes[u] = stage.tile([P, 2, UW], U32, align_bytes=64, name="hcodes")
+            hscales[u] = stage.tile([P, 2, UW], U8, align_bytes=64, name="hscales")
+            nc.vector.quantize_mx(
+                out=hcodes[u][:].rearrange("q g w -> q (g w)").bitcast(FP8X4),
+                scales=hscales[u][:].rearrange("q g w -> q (g w)"),
+                in_=hgrp[u][:].rearrange("q g w x -> q (g w x)"),
+            )
+
+        def stage1(u, jl):
+            cols = slice(jl * P, (jl + 1) * P)
+            z_ps[u, jl] = psum.tile([P, 4, P], F32, name="z%d" % jl)
+            for t in range(4):
+                for g in range(2):
                     nc.tensor.matmul_mx(
-                        out=w_ps[:],
-                        lhsT=zcodes[:, cols].bitcast(FP8X4),
-                        lhsT_scale=zscales[:, cols],
-                        rhs=cwcodes[:, c, :].bitcast(FP8X4),
-                        rhs_scale=cwscales[:, c, :],
-                        start=True,
-                        stop=True,
+                        out=z_ps[u, jl][:, t, :],
+                        lhsT=w3codes[:, g, t * P:(t + 1) * P].bitcast(FP8X4),
+                        lhsT_scale=w3scales[:, g, t * P:(t + 1) * P],
+                        rhs=hcodes[u][:, g, cols].bitcast(FP8X4),
+                        rhs_scale=hscales[u][:, g, cols],
+                        start=(g == 0),
+                        stop=(g == 1),
                     )
-                    diff = dpool.tile([P, E], F32)
-                    nc.vector.tensor_tensor(out=diff[:], in0=w_ps[:], in1=cent_bc[:, c * E:(c + 1) * E], op=ALU.subtract)
-                    nc.scalar.activation(out=diff[:], in_=diff[:], func=ACT.Square, accum_out=dist[:, j, c:c + 1])
 
+        def z_out(u, jl):
+            if jl == 0:
+                zgrp[u] = stage.tile([P, UW, 4], BF16, align_bytes=64, name="zgrp")
+            nc.vector.tensor_tensor(
+                out=zgrp[u][:, jl * P:(jl + 1) * P, :],
+                in0=z_ps[u, jl][:].rearrange("m t b -> m b t"),
+                in1=bias_f[:].unsqueeze(1).to_broadcast([P, P, 4]),
+                op=ALU.add,
+            )
+
+        def z_quantise(u):
+            zcodes[u] = stage.tile([P, UW], U32, align_bytes=64, name="zcodes")
+            zscales[u] = stage.tile([P, UW], U8, align_bytes=64, name="zscales")
+            nc.vector.quantize_mx(
+                out=zcodes[u][:].bitcast(FP8X4),
+                scales=zscales[u][:],
+                in_=zgrp[u][:].rearrange("m b t -> m (b t)"),
+            )
+
+        BANK = ("wb0", "wb1", "wd")
+
+        def rows_mm(u, jl, c):
+            cols = slice(jl * P, (jl + 1) * P)
+            w_ps[u, jl, c] = psum.tile([P, E], F32, name=BANK[c])
+            nc.tensor.matmul_mx(
+                out=w_ps[u, jl, c][:],
+                lhsT=zcodes[u][:, cols].bitcast(FP8X4),
+                lhsT_scale=zscales[u][:, cols],
+                rhs=cwcodes[:, c, :].bitcast(FP8X4),
+                rhs_scale=cwscales[:, c, :],
+                start=True,
+                stop=True,
+            )
+
+        def rows_sub(u, jl, c):
+            diff[u, jl, c] = dpool.tile([P, E], F32, name="diff")
+            nc.vector.tensor_tensor(out=diff[u, jl, c][:], in0=w_ps[u, jl, c][:], in1=cent_bc[:, c, :], op=ALU.subtract)
+
+        def rows_square(u, jl, c):
+            j = u * UNIT + jl
+            nc.scalar.activation(out=diff[u, jl, c][:], in_=diff[u, jl, c][:], func=ACT.Square, accum_out=dist[:, c, j:j + 1])
+
+        def cols_mm(u, pair):
+            wd_ps[u, pair] = psum.tile([P, 2, UW], F32, name="wd")
+            for i in range(2):
+                k = 2 * pair + i
+                nc.tensor.matmul_mx(
+                    out=wd_ps[u, pair][:, i, :],
+                    lhsT=cwcodes[:, CD, k * P:(k + 1) * P].bitcast(FP8X4),
+                    lhsT_scale=cwscales[:, CD, k * P:(k + 1) * P],
+                    rhs=zcodes[u][:].bitcast(FP8X4),
+                    rhs_scale=zscales[u][:],
+                    start=True,
+                    stop=True,
+                )
+
+        def cols_square(u, pair):
+            if pair == 0:
+                sq[u] = sqpool.tile([P, 4, UW], F32, name="sq")
+            for i in range(2):
+                k = 2 * pair + i
+                nc.scalar.activation(out=sq[u][:, k, :], in_=wd_ps[u, pair][:, i, :], func=ACT.Square, bias=negcent[:, k:k + 1])
+
+        def cols_add(u):
+            nc.gpsimd.tensor_tensor(out=sq[u][:, 0:2, :], in0=sq[u][:, 0:2, :], in1=sq[u][:, 2:4, :], op=ALU.add)
+            nc.gpsimd.tensor_tensor(out=sq[u][:, 0, :], in0=sq[u][:, 0, :], in1=sq[u][:, 1, :], op=ALU.add)
+
+        def cols_reduce(u):
+            for jl in range(UNIT):
+                j = u * UNIT + jl
+                nc.tensor.matmul(out=dist_ps[:, j:j + 1], lhsT=sq[u][:, 0, jl * P:(jl + 1) * P], rhs=ones[:], start=True, stop=True)
+
+        def ok(u):
+            return 0 <= u < N_UNITS
+
+        V_COPY, S_COPY = nc.vector.tensor_copy, nc.scalar.copy
+        CW_SPLIT = 320
+        cent_bc = const.tile([P, C, E], F32)
+        negcent = const.tile([P, 4], F32)
+        bias_f = const.tile([P, 4], F32)
+
+        transposes(0)
+        h_out(0, 0, S_COPY)
+        w3_regroup(V_COPY, 0, 0, 3)
+        w3_regroup(S_COPY, 0, 3, 4)
+        h_out(0, 1, S_COPY)
+        w3_regroup(V_COPY, 1, 0, 3)
+        w3_regroup(S_COPY, 1, 3, 4)
+        w3_quantise(0)
+        w3_quantise(1)
+        h_quantise(0)
+
+        for c in range(C):
+            cb_ps = psum.tile([P, E], F32, name=BANK[c])
+            for k in range(4):
+                r = 4 * c + k
+                nc.tensor.matmul(out=cb_ps[:, k * P:(k + 1) * P], lhsT=ident_bf[:, r:r + 1].to_broadcast([P, P]), rhs=crow[:], start=True, stop=True)
+            nc.scalar.copy(out=cent_bc[:, c, :], in_=cb_ps[:])
+        cc_ps = psum.tile([P, 4, P], F32, name="z0")
+        nc.tensor.matmul(out=cc_ps[:, 0, 0:4], lhsT=crow[:], rhs=ident_bf[:, 4 * CD:4 * CD + 4], start=True, stop=True)
+        nc.vector.tensor_scalar(out=negcent[:], in0=cc_ps[:, 0, 0:4], scalar1=-1.0, scalar2=None, op0=ALU.mult)
+        nc.vector.tensor_copy(out=bias_f[:], in_=bias_bf[:])
+
+        transposes(1)
+        h_out(1, 0, S_COPY)
+        h_out(1, 1, S_COPY)
+        cw_regroup(V_COPY, 0, 0, CW_SPLIT)
+        cw_regroup(S_COPY, 0, CW_SPLIT, E)
+        stage1(0, 0)
+        stage1(0, 1)
+        h_quantise(1)
+
+        transposes(2)
+        cw_regroup(V_COPY, 1, 0, CW_SPLIT)
+        cw_regroup(S_COPY, 1, CW_SPLIT, E)
+        h_out(2, 0, S_COPY)
+        h_out(2, 1, S_COPY)
+        z_out(0, 0)
+        z_out(0, 1)
+        cw_quantise(0)
+        cw_regroup(V_COPY, 2, 0, CW_SPLIT)
+        cw_regroup(S_COPY, 2, CW_SPLIT, E)
+        cw_quantise(1)
+        z_quantise(0)
+        cw_quantise(2)
+        stage1(1, 0)
+        stage1(1, 1)
+        rows_mm(0, 0, 0)
+
+        for i in range(N_UNITS - 1):
+            on_vector = i % 2 == 0
+            if ok(i + 4):
+                load_h(i + 4)
+            rows_sub(i, 0, 0)
+            rows_square(i, 0, 0)
+            if ok(i + 2):
+                h_quantise(i + 2)
+            rows_mm(i, 0, 1)
+            cols_mm(i, 0)
+            cols_square(i, 0)
+            z_out(i + 1, 0)
+            rows_mm(i, 1, 0)
+            if ok(i + 3):
+                transposes(i + 3)
+                h_out(i + 3, 0, S_COPY)
+            rows_sub(i, 0, 1)
+            rows_square(i, 0, 1)
+            if ok(i + 2):
+                stage1(i + 2, 0)
+            z_out(i + 1, 1)
+            if ok(i + 3) and not on_vector:
+                h_out(i + 3, 1, S_COPY)
+            rows_sub(i, 1, 0)
+            rows_square(i, 1, 0)
+            z_quantise(i + 1)
+            if ok(i + 3) and on_vector:
+                h_out(i + 3, 1, V_COPY)
+            rows_mm(i, 1, 1)
+            rows_sub(i, 1, 1)
+            cols_mm(i, 1)
+            cols_square(i, 1)
+            rows_square(i, 1, 1)
+            if ok(i + 2):
+                stage1(i + 2, 1)
+            if ok(i - 1):
+                cols_reduce(i - 1)
+            rows_mm(i + 1, 0, 0)
+            cols_add(i)
+
+        last = N_UNITS - 1
+        for jl in range(UNIT):
+            for c in range(C):
+                if (jl, c) != (0, 0):
+                    rows_mm(last, jl, c)
+                rows_sub(last, jl, c)
+                if (jl, c) == (1, 1):
+                    cols_reduce(last - 1)
+                if (jl, c) == (1, 2):
+                    nc.scalar.copy(out=dist[:, CD, 0:last * UNIT], in_=dist_ps[:, 0:last * UNIT])
+                rows_square(last, jl, c)
+
+        dv = dist[:].rearrange("p c j -> p j c")
         neg = -1.0 / (2.0 * LS * LS)
-        kv = const.tile([P, J, C], F32)
-        nc.scalar.activation(out=kv[:], in_=dist[:], func=ACT.Exp, scale=neg)
-        nc.sync.dma_start(out=out_2.rearrange("(p j) c -> p j c", j=J), in_=kv[:])
         dmin = const.tile([P, J], F32)
-        nc.vector.tensor_reduce(out=dmin[:], in_=dist[:], axis=AX.X, op=ALU.min)
+        nc.vector.tensor_reduce(out=dmin[:], in_=dv, axis=AX.X, op=ALU.min)
+        kv = const.tile([P, J, C], F32)
+        nc.scalar.activation(out=kv[:], in_=dv, func=ACT.Exp, scale=neg)
+        nc.sync.dma_start(out=out_2.rearrange("(p j) c -> p j c", j=J), in_=kv[:])
         shifted = const.tile([P, J, C], F32)
-        nc.vector.tensor_tensor(out=shifted[:], in0=dist[:], in1=dmin[:].unsqueeze(2).to_broadcast([P, J, C]), op=ALU.subtract)
+        nc.vector.tensor_tensor(out=shifted[:], in0=dv, in1=dmin[:].unsqueeze(2).to_broadcast([P, J, C]), op=ALU.subtract)
         ex = const.tile([P, J, C], F32)
         nc.scalar.activation(out=ex[:], in_=shifted[:], func=ACT.Exp, scale=neg)
+        kmax = const.tile([P, J], F32)
+        nc.vector.tensor_reduce(out=kmax[:], in_=kv[:], axis=AX.X, op=ALU.max)
+        unc = const.tile([P, J], F32)
+        nc.vector.tensor_scalar(out=unc[:], in0=kmax[:], scalar1=-1.0, scalar2=1.0, op0=ALU.mult, op1=ALU.add)
+        nc.sync.dma_start(out=out_3.rearrange("(p j) -> p j", j=J), in_=unc[:])
         ssum = const.tile([P, J], F32)
         nc.vector.tensor_reduce(out=ssum[:], in_=ex[:], axis=AX.X, op=ALU.add)
         rsum = const.tile([P, J], F32)
@@ -195,8 +356,3 @@ def tile_duqhead_pa_t_kernel(tc, h, W3, b3, class_weight, centroids, out_0, out_
         nc.vector.tensor_tensor(out=probs[:], in0=ex[:], in1=rsum[:].unsqueeze(2).to_broadcast([P, J, C]), op=ALU.mult)
         nc.sync.dma_start(out=out_0.rearrange("(p j) c -> p j c", j=J), in_=probs[:])
         nc.scalar.dma_start(out=out_1.rearrange("o (p j) c -> (o p) j c", j=J), in_=probs[:])
-        kmax = const.tile([P, J], F32)
-        nc.vector.tensor_reduce(out=kmax[:], in_=kv[:], axis=AX.X, op=ALU.max)
-        unc = const.tile([P, J], F32)
-        nc.vector.tensor_scalar(out=unc[:], in0=kmax[:], scalar1=-1.0, scalar2=1.0, op0=ALU.mult, op1=ALU.add)
-        nc.scalar.dma_start(out=out_3.rearrange("(p j) -> p j", j=J), in_=unc[:])

@@ -28,10 +28,10 @@ def tile_duqhead_pa_t_kernel(tc, h, W3, b3, class_weight, centroids, out_0, out_
     with ExitStack() as ctx:
         ctx.enter_context(tc.manual_schedule())
         const = ctx.enter_context(tc.tile_pool(name="const", bufs=1))
-        hpool = ctx.enter_context(tc.tile_pool(name="hpool", bufs=5))
+        hpool = ctx.enter_context(tc.tile_pool(name="hpool", bufs=6))
         stage = ctx.enter_context(tc.tile_pool(name="stage", bufs=2))
         dpool = ctx.enter_context(tc.tile_pool(name="dpool", bufs=6))
-        sqpool = ctx.enter_context(tc.tile_pool(name="sqpool", bufs=3))
+        sqpool = ctx.enter_context(tc.tile_pool(name="sqpool", bufs=4))
         psum = ctx.enter_context(tc.psum_pool(name="psum", bufs=1))
 
         crow = const.tile([P, P], BF16)
@@ -59,6 +59,7 @@ def tile_duqhead_pa_t_kernel(tc, h, W3, b3, class_weight, centroids, out_0, out_
             nc.sync.dma_start(out=cwraw[:, c], in_=cw_view[:, c])
         load_h(2)
         load_h(3)
+        load_h(4)
 
         ident = const.tile([P, P], F32)
         make_identity(nc, ident[:])
@@ -121,7 +122,7 @@ def tile_duqhead_pa_t_kernel(tc, h, W3, b3, class_weight, centroids, out_0, out_
 
         def h_out(u, jl, eng_copy):
             if jl == 0:
-                hgrp[u] = stage.tile([P, 2, UW, 4], BF16, align_bytes=64, name="hgrp")
+                hgrp[u] = stage.tile([P, 2, UW, 4], BF16, align_bytes=64, name="hgrp", bufs=3)
             eng_copy(
                 out=hgrp[u][:].bitcast(F32)[:, :, jl * P:(jl + 1) * P, :],
                 in_=xt[u, jl][:].rearrange("q (g u) w -> q g w u", g=2),
@@ -214,7 +215,9 @@ def tile_duqhead_pa_t_kernel(tc, h, W3, b3, class_weight, centroids, out_0, out_
                 k = 2 * pair + i
                 nc.scalar.activation(out=sq[u][:, k, :], in_=wd_ps[u, pair][:, i, :], func=ACT.Square, bias=negcent[:, k:k + 1])
 
-        def cols_add(u):
+        def cols_add(u, after):
+            if after is not None:
+                nc.gpsimd.tensor_copy(out=gwait[:], in_=after[:, 0, 0:1].bitcast(F32))
             nc.gpsimd.tensor_tensor(out=sq[u][:, 0:2, :], in0=sq[u][:, 0:2, :], in1=sq[u][:, 2:4, :], op=ALU.add)
             nc.gpsimd.tensor_tensor(out=sq[u][:, 0, :], in0=sq[u][:, 0, :], in1=sq[u][:, 1, :], op=ALU.add)
 
@@ -231,6 +234,7 @@ def tile_duqhead_pa_t_kernel(tc, h, W3, b3, class_weight, centroids, out_0, out_
         cent_bc = const.tile([P, C, E], F32)
         negcent = const.tile([P, 4], F32)
         bias_f = const.tile([P, 4], F32)
+        gwait = const.tile([P, 1], F32)
 
         transposes(0)
         h_out(0, 0, S_COPY)
@@ -279,35 +283,38 @@ def tile_duqhead_pa_t_kernel(tc, h, W3, b3, class_weight, centroids, out_0, out_
         stage1(1, 0)
         stage1(1, 1)
         rows_mm(0, 0, 0)
+        h_quantise(2)
+        transposes(3)
+        h_out(3, 0, S_COPY)
+        h_out(3, 1, S_COPY)
 
         for i in range(N_UNITS - 1):
-            on_vector = i % 2 == 0
-            if ok(i + 4):
-                load_h(i + 4)
+            if ok(i + 5):
+                load_h(i + 5)
             rows_sub(i, 0, 0)
             rows_square(i, 0, 0)
-            if ok(i + 2):
-                h_quantise(i + 2)
             rows_mm(i, 0, 1)
             cols_mm(i, 0)
             cols_square(i, 0)
             z_out(i + 1, 0)
             rows_mm(i, 1, 0)
-            if ok(i + 3):
-                transposes(i + 3)
-                h_out(i + 3, 0, S_COPY)
+            if ok(i + 4):
+                transposes(i + 4)
+                h_out(i + 4, 0, S_COPY)
             rows_sub(i, 0, 1)
             rows_square(i, 0, 1)
             if ok(i + 2):
                 stage1(i + 2, 0)
             z_out(i + 1, 1)
-            if ok(i + 3) and not on_vector:
-                h_out(i + 3, 1, S_COPY)
+            if ok(i + 4):
+                h_out(i + 4, 1, S_COPY)
             rows_sub(i, 1, 0)
             rows_square(i, 1, 0)
             z_quantise(i + 1)
-            if ok(i + 3) and on_vector:
-                h_out(i + 3, 1, V_COPY)
+            if ok(i + 3):
+                h_quantise(i + 3)
+            if ok(i - 1):
+                cols_add(i - 1, hcodes[i + 3] if ok(i + 3) else None)
             rows_mm(i, 1, 1)
             rows_sub(i, 1, 1)
             cols_mm(i, 1)
@@ -315,10 +322,9 @@ def tile_duqhead_pa_t_kernel(tc, h, W3, b3, class_weight, centroids, out_0, out_
             rows_square(i, 1, 1)
             if ok(i + 2):
                 stage1(i + 2, 1)
-            if ok(i - 1):
-                cols_reduce(i - 1)
+            if ok(i - 2):
+                cols_reduce(i - 2)
             rows_mm(i + 1, 0, 0)
-            cols_add(i)
 
         last = N_UNITS - 1
         for jl in range(UNIT):
@@ -326,11 +332,14 @@ def tile_duqhead_pa_t_kernel(tc, h, W3, b3, class_weight, centroids, out_0, out_
                 if (jl, c) != (0, 0):
                     rows_mm(last, jl, c)
                 rows_sub(last, jl, c)
-                if (jl, c) == (1, 1):
-                    cols_reduce(last - 1)
+                if (jl, c) == (1, 0):
+                    cols_reduce(last - 2)
                 if (jl, c) == (1, 2):
+                    cols_reduce(last - 1)
                     nc.scalar.copy(out=dist[:, CD, 0:last * UNIT], in_=dist_ps[:, 0:last * UNIT])
                 rows_square(last, jl, c)
+                if (jl, c) == (0, 0):
+                    cols_add(last - 1, None)
 
         dv = dist[:].rearrange("p c j -> p j c")
         neg = -1.0 / (2.0 * LS * LS)

@@ -291,40 +291,41 @@ def tile_duqhead_pa_t_kernel(tc, h, W3, b3, class_weight, centroids, out_0, out_
         for i in range(N_UNITS - 1):
             if ok(i + 5):
                 load_h(i + 5)
-            rows_sub(i, 0, 0)
-            rows_square(i, 0, 0)
             rows_mm(i, 0, 1)
             cols_mm(i, 0)
-            cols_square(i, 0)
             z_out(i + 1, 0)
-            rows_mm(i, 1, 0)
-            if ok(i + 4):
-                transposes(i + 4)
-                h_out(i + 4, 0, S_COPY)
-            rows_sub(i, 0, 1)
-            rows_square(i, 0, 1)
+            rows_sub(i, 0, 0)
             if ok(i + 2):
                 stage1(i + 2, 0)
+            rows_mm(i, 1, 0)
             z_out(i + 1, 1)
+            cols_square(i, 0)
+            rows_square(i, 0, 0)
+            rows_sub(i, 0, 1)
+            rows_square(i, 0, 1)
             if ok(i + 4):
-                h_out(i + 4, 1, S_COPY)
-            rows_sub(i, 1, 0)
-            rows_square(i, 1, 0)
+                transposes(i + 4)
+            rows_mm(i, 1, 1)
+            cols_mm(i, 1)
+            if ok(i + 4):
+                h_out(i + 4, 0, S_COPY)
             z_quantise(i + 1)
             if ok(i + 3):
                 h_quantise(i + 3)
             if ok(i - 1):
                 cols_add(i - 1, hcodes[i + 3] if ok(i + 3) else None)
-            rows_mm(i, 1, 1)
+            rows_sub(i, 1, 0)
             rows_sub(i, 1, 1)
-            cols_mm(i, 1)
             cols_square(i, 1)
-            rows_square(i, 1, 1)
-            if ok(i + 2):
-                stage1(i + 2, 1)
+            rows_square(i, 1, 0)
             if ok(i - 2):
                 cols_reduce(i - 2)
             rows_mm(i + 1, 0, 0)
+            if ok(i + 4):
+                h_out(i + 4, 1, S_COPY)
+            if ok(i + 2):
+                stage1(i + 2, 1)
+            rows_square(i, 1, 1)
 
         last = N_UNITS - 1
         for jl in range(UNIT):

@@ -188,7 +188,7 @@ def tile_duqhead_pa_t_kernel(tc, h, W3, b3, class_weight, centroids, out_0, out_
 
         def rows_sub(u, jl, c):
             diff[u, jl, c] = dpool.tile([P, E], F32, name="diff")
-            nc.vector.tensor_tensor(out=diff[u, jl, c][:], in0=w_ps[u, jl, c][:], in1=cent_bc[:, c, :], op=ALU.subtract)
+            nc.vector.tensor_tensor(out=diff[u, jl, c][:], in0=w_ps[u, jl, c][:], in1=cent_last[:] if c == CD else cent_bc[:, c, :], op=ALU.subtract)
 
         def rows_square(u, jl, c):
             j = u * UNIT + jl
@@ -230,11 +230,19 @@ def tile_duqhead_pa_t_kernel(tc, h, W3, b3, class_weight, centroids, out_0, out_
             return 0 <= u < N_UNITS
 
         V_COPY, S_COPY = nc.vector.tensor_copy, nc.scalar.copy
-        CW_SPLIT = 320
-        cent_bc = const.tile([P, C, E], F32)
+        CW_SPLIT = 256
+        cent_bc = const.tile([P, CD, E], F32)
+        cent_last = const.tile([P, E], BF16)
         negcent = const.tile([P, 4], F32)
         bias_f = const.tile([P, 4], F32)
         gwait = const.tile([P, 1], F32)
+
+        def centroid_rows(c):
+            cb_ps = psum.tile([P, E], F32, name=BANK[c])
+            for k in range(4):
+                r = 4 * c + k
+                nc.tensor.matmul(out=cb_ps[:, k * P:(k + 1) * P], lhsT=ident_bf[:, r:r + 1].to_broadcast([P, P]), rhs=crow[:], start=True, stop=True)
+            nc.scalar.copy(out=cent_bc[:, c, :], in_=cb_ps[:])
 
         transposes(0)
         h_out(0, 0, S_COPY)
@@ -245,52 +253,48 @@ def tile_duqhead_pa_t_kernel(tc, h, W3, b3, class_weight, centroids, out_0, out_
         w3_regroup(S_COPY, 1, 3, 4)
         w3_quantise(0)
         w3_quantise(1)
-        h_quantise(0)
-
-        for c in range(C):
-            cb_ps = psum.tile([P, E], F32, name=BANK[c])
-            for k in range(4):
-                r = 4 * c + k
-                nc.tensor.matmul(out=cb_ps[:, k * P:(k + 1) * P], lhsT=ident_bf[:, r:r + 1].to_broadcast([P, P]), rhs=crow[:], start=True, stop=True)
-            nc.scalar.copy(out=cent_bc[:, c, :], in_=cb_ps[:])
-        cc_ps = psum.tile([P, 4, P], F32, name="z0")
-        nc.tensor.matmul(out=cc_ps[:, 0, 0:4], lhsT=crow[:], rhs=ident_bf[:, 4 * CD:4 * CD + 4], start=True, stop=True)
-        nc.vector.tensor_scalar(out=negcent[:], in0=cc_ps[:, 0, 0:4], scalar1=-1.0, scalar2=None, op0=ALU.mult)
-        nc.vector.tensor_copy(out=bias_f[:], in_=bias_bf[:])
-
         transposes(1)
+        h_quantise(0)
         h_out(1, 0, S_COPY)
         h_out(1, 1, S_COPY)
         cw_regroup(V_COPY, 0, 0, CW_SPLIT)
         cw_regroup(S_COPY, 0, CW_SPLIT, E)
-        stage1(0, 0)
-        stage1(0, 1)
         h_quantise(1)
 
-        transposes(2)
+        cc_ps = psum.tile([P, 2, UW], F32, name="wd")
+        nc.tensor.matmul(out=cc_ps[:, 0, 0:4], lhsT=crow[:], rhs=ident_bf[:, 4 * CD:4 * CD + 4], start=True, stop=True)
+        nc.vector.tensor_scalar(out=negcent[:], in0=cc_ps[:, 0, 0:4], scalar1=-1.0, scalar2=None, op0=ALU.mult)
+        nc.vector.tensor_copy(out=bias_f[:], in_=bias_bf[:])
+        stage1(0, 0)
+        stage1(0, 1)
         cw_regroup(V_COPY, 1, 0, CW_SPLIT)
         cw_regroup(S_COPY, 1, CW_SPLIT, E)
+        cw_regroup(S_COPY, 2, CW_SPLIT, E)
+        centroid_rows(0)
+        transposes(2)
         h_out(2, 0, S_COPY)
         h_out(2, 1, S_COPY)
+        centroid_rows(1)
         z_out(0, 0)
         z_out(0, 1)
         cw_quantise(0)
         cw_regroup(V_COPY, 2, 0, CW_SPLIT)
-        cw_regroup(S_COPY, 2, CW_SPLIT, E)
         cw_quantise(1)
         z_quantise(0)
         cw_quantise(2)
         stage1(1, 0)
         stage1(1, 1)
+        transposes(3)
         rows_mm(0, 0, 0)
         h_quantise(2)
-        transposes(3)
         h_out(3, 0, S_COPY)
         h_out(3, 1, S_COPY)
 
         for i in range(N_UNITS - 1):
             if ok(i + 5):
                 load_h(i + 5)
+            if i == N_UNITS - 5:
+                nc.sync.dma_start(out=cent_last[:], in_=centroids[CD:CD + 1, :].rearrange("o d -> (o d)").partition_broadcast(P))
             rows_mm(i, 0, 1)
             cols_mm(i, 0)
             z_out(i + 1, 0)
@@ -322,7 +326,7 @@ def tile_duqhead_pa_t_kernel(tc, h, W3, b3, class_weight, centroids, out_0, out_
                 cols_reduce(i - 2)
             rows_mm(i + 1, 0, 0)
             if ok(i + 4):
-                h_out(i + 4, 1, S_COPY)
+                h_out(i + 4, 1, V_COPY if i % 4 == 3 else S_COPY)
             if ok(i + 2):
                 stage1(i + 2, 1)
             rows_square(i, 1, 1)

@@ -57,7 +57,8 @@ def tile_duqhead_pa_t_kernel(tc, h, W3, b3, class_weight, centroids, out_0, out_
         cw_view = class_weight.rearrange("c (p j) d -> p c j d", j=4)
         for c in range(C):
             nc.sync.dma_start(out=cwraw[:, c], in_=cw_view[:, c])
-        load_h(2)
+            if c == 1:
+                load_h(2)
         load_h(3)
         load_h(4)
 
@@ -173,9 +174,14 @@ def tile_duqhead_pa_t_kernel(tc, h, W3, b3, class_weight, centroids, out_0, out_
 
         BANK = ("wb0", "wb1", "wd")
 
+        def rows_bank(u, jl, c):
+            if jl == 1 and u >= N_UNITS - 4:
+                return ("xt0", "xt1", "z0")[c]
+            return BANK[c]
+
         def rows_mm(u, jl, c):
             cols = slice(jl * P, (jl + 1) * P)
-            w_ps[u, jl, c] = psum.tile([P, E], F32, name=BANK[c])
+            w_ps[u, jl, c] = psum.tile([P, E], F32, name=rows_bank(u, jl, c))
             nc.tensor.matmul_mx(
                 out=w_ps[u, jl, c][:],
                 lhsT=zcodes[u][:, cols].bitcast(FP8X4),
@@ -193,6 +199,10 @@ def tile_duqhead_pa_t_kernel(tc, h, W3, b3, class_weight, centroids, out_0, out_
         def rows_square(u, jl, c):
             j = u * UNIT + jl
             nc.scalar.activation(out=diff[u, jl, c][:], in_=diff[u, jl, c][:], func=ACT.Square, accum_out=dist[:, c, j:j + 1])
+
+        def rows_square_v(u, jl, c):
+            j = u * UNIT + jl
+            nc.vector.scalar_tensor_tensor(out=diff[u, jl, c][:], in0=diff[u, jl, c][:], scalar=1.0, in1=diff[u, jl, c][:], op0=ALU.mult, op1=ALU.mult, accum_out=dist[:, c, j:j + 1])
 
         def cols_mm(u, pair):
             wd_ps[u, pair] = psum.tile([P, 2, UW], F32, name="wd")
@@ -259,7 +269,6 @@ def tile_duqhead_pa_t_kernel(tc, h, W3, b3, class_weight, centroids, out_0, out_
         h_out(1, 1, S_COPY)
         cw_regroup(V_COPY, 0, 0, CW_SPLIT)
         cw_regroup(S_COPY, 0, CW_SPLIT, E)
-        h_quantise(1)
 
         cc_ps = psum.tile([P, 2, UW], F32, name="wd")
         nc.tensor.matmul(out=cc_ps[:, 0, 0:4], lhsT=crow[:], rhs=ident_bf[:, 4 * CD:4 * CD + 4], start=True, stop=True)
@@ -268,12 +277,13 @@ def tile_duqhead_pa_t_kernel(tc, h, W3, b3, class_weight, centroids, out_0, out_
         stage1(0, 0)
         stage1(0, 1)
         cw_regroup(V_COPY, 1, 0, CW_SPLIT)
+        h_quantise(1)
         cw_regroup(S_COPY, 1, CW_SPLIT, E)
-        cw_regroup(S_COPY, 2, CW_SPLIT, E)
-        centroid_rows(0)
         transposes(2)
         h_out(2, 0, S_COPY)
+        cw_regroup(S_COPY, 2, CW_SPLIT, E)
         h_out(2, 1, S_COPY)
+        centroid_rows(0)
         centroid_rows(1)
         z_out(0, 0)
         z_out(0, 1)
@@ -326,7 +336,7 @@ def tile_duqhead_pa_t_kernel(tc, h, W3, b3, class_weight, centroids, out_0, out_
                 cols_reduce(i - 2)
             rows_mm(i + 1, 0, 0)
             if ok(i + 4):
-                h_out(i + 4, 1, V_COPY if i % 4 == 3 else S_COPY)
+                h_out(i + 4, 1, V_COPY if i % 5 == 4 else S_COPY)
             if ok(i + 2):
                 stage1(i + 2, 1)
             rows_square(i, 1, 1)
@@ -337,14 +347,16 @@ def tile_duqhead_pa_t_kernel(tc, h, W3, b3, class_weight, centroids, out_0, out_
                 if (jl, c) != (0, 0):
                     rows_mm(last, jl, c)
                 rows_sub(last, jl, c)
-                if (jl, c) == (1, 0):
-                    cols_reduce(last - 2)
                 if (jl, c) == (1, 2):
+                    cols_reduce(last - 2)
                     cols_reduce(last - 1)
-                    nc.scalar.copy(out=dist[:, CD, 0:last * UNIT], in_=dist_ps[:, 0:last * UNIT])
-                rows_square(last, jl, c)
+                    rows_square_v(last, jl, c)
+                else:
+                    rows_square(last, jl, c)
                 if (jl, c) == (0, 0):
                     cols_add(last - 1, None)
+
+        nc.vector.tensor_copy(out=dist[:, CD, 0:last * UNIT], in_=dist_ps[:, 0:last * UNIT])
 
         dv = dist[:].rearrange("p c j -> p j c")
         neg = -1.0 / (2.0 * LS * LS)

@@ -36,9 +36,7 @@ def tile_duqhead_pa_t_kernel(tc, h, W3, b3, class_weight, centroids, out_0, out_
 
         crow = const.tile([P, P], BF16)
         nc.vector.memset(crow[:], 0.0)
-        nc.scalar.dma_start(out=crow[0:4 * C, :], in_=centroids.rearrange("c (k p) -> (c k) p", p=P))
         bias_bf = const.tile([P, 4], BF16)
-        nc.scalar.dma_start(out=bias_bf[:], in_=b3.rearrange("(m t) -> m t", t=4))
 
         h_view = h.rearrange("(p j) k -> p j k", j=J)
         h_sb = {}
@@ -48,6 +46,8 @@ def tile_duqhead_pa_t_kernel(tc, h, W3, b3, class_weight, centroids, out_0, out_
             nc.sync.dma_start(out=h_sb[u][:], in_=h_view[:, u * UNIT:(u + 1) * UNIT, :])
 
         load_h(0)
+        nc.sync.dma_start(out=crow[0:4 * C, :], in_=centroids.rearrange("c (k p) -> (c k) p", p=P))
+        nc.sync.dma_start(out=bias_bf[:], in_=b3.rearrange("(m t) -> m t", t=4))
         w3raw = const.tile([P, 4, 2 * E], BF16)
         w3_view = W3.rearrange("(a q e) c -> q a (e c)", a=4, q=P, e=2)
         nc.sync.dma_start(out=w3raw[:, 0:2], in_=w3_view[:, 0:2])
@@ -240,7 +240,7 @@ def tile_duqhead_pa_t_kernel(tc, h, W3, b3, class_weight, centroids, out_0, out_
             return 0 <= u < N_UNITS
 
         V_COPY, S_COPY = nc.vector.tensor_copy, nc.scalar.copy
-        CW_SPLIT = 256
+        CW_SPLIT = 192
         cent_bc = const.tile([P, CD, E], F32)
         cent_last = const.tile([P, E], BF16)
         negcent = const.tile([P, 4], F32)
@@ -259,10 +259,11 @@ def tile_duqhead_pa_t_kernel(tc, h, W3, b3, class_weight, centroids, out_0, out_
         w3_regroup(V_COPY, 0, 0, 3)
         w3_regroup(S_COPY, 0, 3, 4)
         h_out(0, 1, S_COPY)
-        w3_regroup(V_COPY, 1, 0, 3)
-        w3_regroup(S_COPY, 1, 3, 4)
+        w3_regroup(V_COPY, 1, 0, 2)
+        w3_regroup(S_COPY, 1, 2, 4)
         w3_quantise(0)
         w3_quantise(1)
+        centroid_rows(0)
         transposes(1)
         h_quantise(0)
         h_out(1, 0, S_COPY)
@@ -283,7 +284,6 @@ def tile_duqhead_pa_t_kernel(tc, h, W3, b3, class_weight, centroids, out_0, out_
         h_out(2, 0, S_COPY)
         cw_regroup(S_COPY, 2, CW_SPLIT, E)
         h_out(2, 1, S_COPY)
-        centroid_rows(0)
         centroid_rows(1)
         z_out(0, 0)
         z_out(0, 1)

@@ -36,7 +36,6 @@ def tile_duqhead_pa_t_kernel(tc, h, W3, b3, class_weight, centroids, out_0, out_
 
         crow = const.tile([P, P], BF16)
         nc.vector.memset(crow[:], 0.0)
-        bias_bf = const.tile([P, 4], BF16)
 
         h_view = h.rearrange("(p j) k -> p j k", j=J)
         h_sb = {}
@@ -47,14 +46,14 @@ def tile_duqhead_pa_t_kernel(tc, h, W3, b3, class_weight, centroids, out_0, out_
 
         load_h(0)
         nc.sync.dma_start(out=crow[0:4 * C, :], in_=centroids.rearrange("c (k p) -> (c k) p", p=P))
-        nc.sync.dma_start(out=bias_bf[:], in_=b3.rearrange("(m t) -> m t", t=4))
+        nc.sync.dma_start(out=crow[4 * C:4 * C + 4, :], in_=b3.rearrange("(k p) -> k p", p=P))
         w3raw = const.tile([P, 4, 2 * E], BF16)
         w3_view = W3.rearrange("(a q e) c -> q a (e c)", a=4, q=P, e=2)
         nc.sync.dma_start(out=w3raw[:, 0:2], in_=w3_view[:, 0:2])
         nc.sync.dma_start(out=w3raw[:, 2:4], in_=w3_view[:, 2:4])
         load_h(1)
         cwraw = const.tile([P, C, 4, E], BF16)
-        cw_view = class_weight.rearrange("c (p j) d -> p c j d", j=4)
+        cw_view = class_weight.rearrange("c (j p) d -> p c j d", j=4)
         for c in range(C):
             nc.sync.dma_start(out=cwraw[:, c], in_=cw_view[:, c])
             if c == 1:
@@ -70,18 +69,18 @@ def tile_duqhead_pa_t_kernel(tc, h, W3, b3, class_weight, centroids, out_0, out_
         nc.scalar.activation(out=warm2[:], in_=warm[:], func=ACT.Exp)
         ones = const.tile([P, 1], F32)
         nc.vector.memset(ones[:], 1.0)
-        ident_bf = const.tile([P, 4 * C], BF16)
-        nc.vector.tensor_copy(out=ident_bf[:], in_=ident[:, 0:4 * C])
+        ident_bf = const.tile([P, 4 * C + 4], BF16)
+        nc.vector.tensor_copy(out=ident_bf[:], in_=ident[:, 0:4 * C + 4])
 
 
         w3grp = const.tile([P, 2, E, 4], BF16, align_bytes=64)
         w3codes = const.tile([P, 2, E], U32, align_bytes=64)
         w3scales = const.tile([P, 2, E], U8, align_bytes=64)
 
-        def w3_regroup(eng_copy, g, t0, t1):
-            src = w3raw[:, 2 * g:2 * g + 2, :].rearrange("q u (e m t) -> q t m (u e)", e=2, t=4)
-            dst = w3grp[:, g].rearrange("q (t m) x -> q t m x", t=4)
-            eng_copy(out=dst[:, t0:t1], in_=src[:, t0:t1])
+        def w3_regroup(eng_copy, g, d0, d1):
+            src = w3raw[:, 2 * g:2 * g + 2, :].rearrange("q u (e a i) -> q a (u e) i", e=2, i=4)
+            dst = w3grp[:, g].rearrange("q (a i) x -> q a x i", i=4)
+            eng_copy(out=dst[:, d0 // 4:d1 // 4], in_=src[:, d0 // 4:d1 // 4])
 
         def w3_quantise(g):
             nc.vector.quantize_mx(
@@ -240,6 +239,7 @@ def tile_duqhead_pa_t_kernel(tc, h, W3, b3, class_weight, centroids, out_0, out_
             return 0 <= u < N_UNITS
 
         V_COPY, S_COPY = nc.vector.tensor_copy, nc.scalar.copy
+        W3_SPLIT = (384, 256)
         CW_SPLIT = 192
         cent_bc = const.tile([P, CD, E], F32)
         cent_last = const.tile([P, E], BF16)
@@ -256,11 +256,11 @@ def tile_duqhead_pa_t_kernel(tc, h, W3, b3, class_weight, centroids, out_0, out_
 
         transposes(0)
         h_out(0, 0, S_COPY)
-        w3_regroup(V_COPY, 0, 0, 3)
-        w3_regroup(S_COPY, 0, 3, 4)
+        w3_regroup(V_COPY, 0, 0, W3_SPLIT[0])
+        w3_regroup(S_COPY, 0, W3_SPLIT[0], E)
         h_out(0, 1, S_COPY)
-        w3_regroup(V_COPY, 1, 0, 2)
-        w3_regroup(S_COPY, 1, 2, 4)
+        w3_regroup(V_COPY, 1, 0, W3_SPLIT[1])
+        w3_regroup(S_COPY, 1, W3_SPLIT[1], E)
         w3_quantise(0)
         w3_quantise(1)
         centroid_rows(0)
@@ -272,9 +272,9 @@ def tile_duqhead_pa_t_kernel(tc, h, W3, b3, class_weight, centroids, out_0, out_
         cw_regroup(S_COPY, 0, CW_SPLIT, E)
 
         cc_ps = psum.tile([P, 2, UW], F32, name="wd")
-        nc.tensor.matmul(out=cc_ps[:, 0, 0:4], lhsT=crow[:], rhs=ident_bf[:, 4 * CD:4 * CD + 4], start=True, stop=True)
+        nc.tensor.matmul(out=cc_ps[:, 0, 0:8], lhsT=crow[:], rhs=ident_bf[:, 4 * CD:4 * CD + 8], start=True, stop=True)
         nc.vector.tensor_scalar(out=negcent[:], in0=cc_ps[:, 0, 0:4], scalar1=-1.0, scalar2=None, op0=ALU.mult)
-        nc.vector.tensor_copy(out=bias_f[:], in_=bias_bf[:])
+        nc.vector.tensor_copy(out=bias_f[:], in_=cc_ps[:, 0, 4:8])
         stage1(0, 0)
         stage1(0, 1)
         cw_regroup(V_COPY, 1, 0, CW_SPLIT)

@@ -240,7 +240,7 @@ def tile_duqhead_pa_t_kernel(tc, h, W3, b3, class_weight, centroids, out_0, out_
 
         V_COPY, S_COPY = nc.vector.tensor_copy, nc.scalar.copy
         W3_SPLIT = (384, 256)
-        CW_SPLIT = 192
+        CW_SPLIT = 256
         cent_bc = const.tile([P, CD, E], F32)
         cent_last = const.tile([P, E], BF16)
         negcent = const.tile([P, 4], F32)

@@ -336,7 +336,7 @@ def tile_duqhead_pa_t_kernel(tc, h, W3, b3, class_weight, centroids, out_0, out_
                 cols_reduce(i - 2)
             rows_mm(i + 1, 0, 0)
             if ok(i + 4):
-                h_out(i + 4, 1, V_COPY if i % 5 == 4 else S_COPY)
+                h_out(i + 4, 1, V_COPY if i % 4 == 2 else S_COPY)
             if ok(i + 2):
                 stage1(i + 2, 1)
             rows_square(i, 1, 1)

from contextlib import ExitStack

import concourse.mybir as mybir
from concourse.masks import make_identity

F32 = mybir.dt.float32
BF16 = mybir.dt.bfloat16
U32 = mybir.dt.uint32
U8 = mybir.dt.uint8
FP8X4 = mybir.dt.float8_e4m3fn_x4
ALU = mybir.AluOpType
ACT = mybir.ActivationFunctionType
AX = mybir.AxisListType

P = 128
B, HIDDEN, E, C = 4096, 1024, 512, 3
LS = 0.1
J = B // P
UNIT = 2
UW = UNIT * P
N_UNITS = J // UNIT
CD = 2
FLOPS = 2 * B * HIDDEN * E + 2 * B * E * C * E


def tile_duqhead_pa_t_kernel(tc, h, W3, b3, class_weight, centroids, out_0, out_1, out_2, out_3):
    nc = tc.nc
    with ExitStack() as ctx:
        ctx.enter_context(tc.manual_schedule())
        const = ctx.enter_context(tc.tile_pool(name="const", bufs=1))
        hpool = ctx.enter_context(tc.tile_pool(name="hpool", bufs=6))
        stage = ctx.enter_context(tc.tile_pool(name="stage", bufs=2))
        dpool = ctx.enter_context(tc.tile_pool(name="dpool", bufs=6))
        sqpool = ctx.enter_context(tc.tile_pool(name="sqpool", bufs=4))
        psum = ctx.enter_context(tc.psum_pool(name="psum", bufs=1))

        crow = const.tile([P, P], BF16)
        nc.vector.memset(crow[:], 0.0)

        h_view = h.rearrange("(p j) k -> p j k", j=J)
        h_sb = {}

        def load_h(u):
            h_sb[u] = hpool.tile([P, UNIT, HIDDEN], BF16, name="h_sb")
            nc.sync.dma_start(out=h_sb[u][:], in_=h_view[:, u * UNIT:(u + 1) * UNIT, :])

        load_h(0)
        nc.sync.dma_start(out=crow[0:4 * C, :], in_=centroids.rearrange("c (k p) -> (c k) p", p=P))
        nc.sync.dma_start(out=crow[4 * C:4 * C + 4, :], in_=b3.rearrange("(k p) -> k p", p=P))
        w3raw = const.tile([P, 4, 2 * E], BF16)
        w3_view = W3.rearrange("(a q e) c -> q a (e c)", a=4, q=P, e=2)
        nc.sync.dma_start(out=w3raw[:, 0:2], in_=w3_view[:, 0:2])
        nc.sync.dma_start(out=w3raw[:, 2:4], in_=w3_view[:, 2:4])
        load_h(1)
        cwraw = const.tile([P, C, 4, E], BF16)
        cw_view = class_weight.rearrange("c (j p) d -> p c j d", j=4)
        for c in range(C):
            nc.sync.dma_start(out=cwraw[:, c], in_=cw_view[:, c])
            if c == 1:
                load_h(2)
        load_h(3)
        load_h(4)

        ident = const.tile([P, P], F32)
        make_identity(nc, ident[:])
        warm = const.tile([P, 1], F32)
        nc.vector.memset(warm[:], 0.0)
        warm2 = const.tile([P, 1], F32)
        nc.scalar.activation(out=warm2[:], in_=warm[:], func=ACT.Exp)
        ones = const.tile([P, 1], F32)
        nc.vector.memset(ones[:], 1.0)
        ident_bf = const.tile([P, 4 * C + 4], BF16)
        nc.vector.tensor_copy(out=ident_bf[:], in_=ident[:, 0:4 * C + 4])


        w3grp = const.tile([P, 2, E, 4], BF16, align_bytes=64)
        w3codes = const.tile([P, 2, E], U32, align_bytes=64)
        w3scales = const.tile([P, 2, E], U8, align_bytes=64)

        def w3_regroup(eng_copy, g, d0, d1):
            src = w3raw[:, 2 * g:2 * g + 2, :].rearrange("q u (e a i) -> q a (u e) i", e=2, i=4)
            dst = w3grp[:, g].rearrange("q (a i) x -> q a x i", i=4)
            eng_copy(out=dst[:, d0 // 4:d1 // 4], in_=src[:, d0 // 4:d1 // 4])

        def w3_quantise(g):
            nc.vector.quantize_mx(
                out=w3codes[:, g, :].bitcast(FP8X4),
                scales=w3scales[:, g, :],
                in_=w3grp[:, g].rearrange("q c x -> q (c x)"),
            )

        cwgrp = const.tile([P, C, E, 4], BF16, align_bytes=64)
        cwcodes = const.tile([P, C, E], U32, align_bytes=64)
        cwscales = const.tile([P, C, E], U8, align_bytes=64)

        def cw_regroup(eng_copy, c, d0, d1):
            eng_copy(
                out=cwgrp[:, c, d0:d1, :].rearrange("p (a i) j -> p a j i", i=4),
                in_=cwraw[:, c, :, d0:d1].rearrange("p j (a i) -> p a j i", i=4),
            )

        def cw_quantise(c):
            nc.vector.quantize_mx(
                out=cwcodes[:, c, :].bitcast(FP8X4),
                scales=cwscales[:, c, :],
                in_=cwgrp[:, c].rearrange("p d j -> p (d j)"),
            )

        dist = const.tile([P, C, J], F32)
        dist_ps = psum.tile([P, J], F32)

        xt, hgrp, hcodes, hscales = {}, {}, {}, {}
        z_ps, zgrp, zcodes, zscales = {}, {}, {}, {}
        w_ps, diff, wd_ps, sq = {}, {}, {}, {}

        def transposes(u):
            words = h_sb[u][:].bitcast(F32)
            for jl in range(UNIT):
                xt[u, jl] = psum.tile([P, 4, P], F32, name="xt%d" % jl)
                for a in range(4):
                    nc.tensor.transpose(xt[u, jl][:, a, :], words[:, jl, a * P:(a + 1) * P], ident[:])

        def h_out(u, jl, eng_copy):
            if jl == 0:
                hgrp[u] = stage.tile([P, 2, UW, 4], BF16, align_bytes=64, name="hgrp", bufs=3)
            eng_copy(
                out=hgrp[u][:].bitcast(F32)[:, :, jl * P:(jl + 1) * P, :],
                in_=xt[u, jl][:].rearrange("q (g u) w -> q g w u", g=2),
            )

        def h_quantise(u):
            hcodes[u] = stage.tile([P, 2, UW], U32, align_bytes=64, name="hcodes")
            hscales[u] = stage.tile([P, 2, UW], U8, align_bytes=64, name="hscales")
            nc.vector.quantize_mx(
                out=hcodes[u][:].rearrange("q g w -> q (g w)").bitcast(FP8X4),
                scales=hscales[u][:].rearrange("q g w -> q (g w)"),
                in_=hgrp[u][:].rearrange("q g w x -> q (g w x)"),
            )

        def stage1(u, jl):
            cols = slice(jl * P, (jl + 1) * P)
            z_ps[u, jl] = psum.tile([P, 4, P], F32, name="z%d" % jl)
            for t in range(4):
                for g in range(2):
                    nc.tensor.matmul_mx(
                        out=z_ps[u, jl][:, t, :],
                        lhsT=w3codes[:, g, t * P:(t + 1) * P].bitcast(FP8X4),
                        lhsT_scale=w3scales[:, g, t * P:(t + 1) * P],
                        rhs=hcodes[u][:, g, cols].bitcast(FP8X4),
                        rhs_scale=hscales[u][:, g, cols],
                        start=(g == 0),
                        stop=(g == 1),
                    )

        def z_out(u, jl):
            if jl == 0:
                zgrp[u] = stage.tile([P, UW, 4], BF16, align_bytes=64, name="zgrp")
            nc.vector.tensor_tensor(
                out=zgrp[u][:, jl * P:(jl + 1) * P, :],
                in0=z_ps[u, jl][:].rearrange("m t b -> m b t"),
                in1=bias_f[:].unsqueeze(1).to_broadcast([P, P, 4]),
                op=ALU.add,
            )

        def z_quantise(u):
            zcodes[u] = stage.tile([P, UW], U32, align_bytes=64, name="zcodes")
            zscales[u] = stage.tile([P, UW], U8, align_bytes=64, name="zscales")
            nc.vector.quantize_mx(
                out=zcodes[u][:].bitcast(FP8X4),
                scales=zscales[u][:],
                in_=zgrp[u][:].rearrange("m b t -> m (b t)"),
            )

        BANK = ("wb0", "wb1", "wd")

        def rows_bank(u, jl, c):
            if jl == 1 and u >= N_UNITS - 4:
                return ("xt0", "xt1", "z0")[c]
            return BANK[c]

        def rows_mm(u, jl, c):
            cols = slice(jl * P, (jl + 1) * P)
            w_ps[u, jl, c] = psum.tile([P, E], F32, name=rows_bank(u, jl, c))
            nc.tensor.matmul_mx(
                out=w_ps[u, jl, c][:],
                lhsT=zcodes[u][:, cols].bitcast(FP8X4),
                lhsT_scale=zscales[u][:, cols],
                rhs=cwcodes[:, c, :].bitcast(FP8X4),
                rhs_scale=cwscales[:, c, :],
                start=True,
                stop=True,
            )

        def rows_sub(u, jl, c):
            diff[u, jl, c] = dpool.tile([P, E], F32, name="diff")
            nc.vector.tensor_tensor(out=diff[u, jl, c][:], in0=w_ps[u, jl, c][:], in1=cent_last[:] if c == CD else cent_bc[:, c, :], op=ALU.subtract)

        def rows_square(u, jl, c):
            j = u * UNIT + jl
            nc.scalar.activation(out=diff[u, jl, c][:], in_=diff[u, jl, c][:], func=ACT.Square, accum_out=dist[:, c, j:j + 1])

        def rows_square_v(u, jl, c):
            j = u * UNIT + jl
            nc.vector.scalar_tensor_tensor(out=diff[u, jl, c][:], in0=diff[u, jl, c][:], scalar=1.0, in1=diff[u, jl, c][:], op0=ALU.mult, op1=ALU.mult, accum_out=dist[:, c, j:j + 1])

        def cols_mm(u, pair):
            wd_ps[u, pair] = psum.tile([P, 2, UW], F32, name="wd")
            for i in range(2):
                k = 2 * pair + i
                nc.tensor.matmul_mx(
                    out=wd_ps[u, pair][:, i, :],
                    lhsT=cwcodes[:, CD, k * P:(k + 1) * P].bitcast(FP8X4),
                    lhsT_scale=cwscales[:, CD, k * P:(k + 1) * P],
                    rhs=zcodes[u][:].bitcast(FP8X4),
                    rhs_scale=zscales[u][:],
                    start=True,
                    stop=True,
                )

        def cols_square(u, pair):
            if pair == 0:
                sq[u] = sqpool.tile([P, 4, UW], F32, name="sq")
            for i in range(2):
                k = 2 * pair + i
                nc.scalar.activation(out=sq[u][:, k, :], in_=wd_ps[u, pair][:, i, :], func=ACT.Square, bias=negcent[:, k:k + 1])

        def cols_add(u, after):
            if after is not None:
                nc.gpsimd.tensor_copy(out=gwait[:], in_=after[:, 0, 0:1].bitcast(F32))
            nc.gpsimd.tensor_tensor(out=sq[u][:, 0:2, :], in0=sq[u][:, 0:2, :], in1=sq[u][:, 2:4, :], op=ALU.add)
            nc.gpsimd.tensor_tensor(out=sq[u][:, 0, :], in0=sq[u][:, 0, :], in1=sq[u][:, 1, :], op=ALU.add)

        def cols_reduce(u):
            for jl in range(UNIT):
                j = u * UNIT + jl
                nc.tensor.matmul(out=dist_ps[:, j:j + 1], lhsT=sq[u][:, 0, jl * P:(jl + 1) * P], rhs=ones[:], start=True, stop=True)

        def ok(u):
            return 0 <= u < N_UNITS

        V_COPY, S_COPY = nc.vector.tensor_copy, nc.scalar.copy
        W3_SPLIT = (384, 256)
        CW_SPLIT = 256
        cent_bc = const.tile([P, CD, E], F32)
        cent_last = const.tile([P, E], BF16)
        negcent = const.tile([P, 4], F32)
        bias_f = const.tile([P, 4], F32)
        gwait = const.tile([P, 1], F32)

        def centroid_rows(c):
            cb_ps = psum.tile([P, E], F32, name=BANK[c])
            for k in range(4):
                r = 4 * c + k
                nc.tensor.matmul(out=cb_ps[:, k * P:(k + 1) * P], lhsT=ident_bf[:, r:r + 1].to_broadcast([P, P]), rhs=crow[:], start=True, stop=True)
            nc.scalar.copy(out=cent_bc[:, c, :], in_=cb_ps[:])

        transposes(0)
        h_out(0, 0, S_COPY)
        w3_regroup(V_COPY, 0, 0, W3_SPLIT[0])
        w3_regroup(S_COPY, 0, W3_SPLIT[0], E)
        h_out(0, 1, S_COPY)
        w3_regroup(V_COPY, 1, 0, W3_SPLIT[1])
        w3_regroup(S_COPY, 1, W3_SPLIT[1], E)
        w3_quantise(0)
        w3_quantise(1)
        centroid_rows(0)
        transposes(1)
        h_quantise(0)
        h_out(1, 0, S_COPY)
        h_out(1, 1, S_COPY)
        cw_regroup(V_COPY, 0, 0, CW_SPLIT)
        cw_regroup(S_COPY, 0, CW_SPLIT, E)

        cc_ps = psum.tile([P, 2, UW], F32, name="wd")
        nc.tensor.matmul(out=cc_ps[:, 0, 0:8], lhsT=crow[:], rhs=ident_bf[:, 4 * CD:4 * CD + 8], start=True, stop=True)
        nc.vector.tensor_scalar(out=negcent[:], in0=cc_ps[:, 0, 0:4], scalar1=-1.0, scalar2=None, op0=ALU.mult)
        nc.vector.tensor_copy(out=bias_f[:], in_=cc_ps[:, 0, 4:8])
        stage1(0, 0)
        stage1(0, 1)
        cw_regroup(V_COPY, 1, 0, CW_SPLIT)
        h_quantise(1)
        cw_regroup(S_COPY, 1, CW_SPLIT, E)
        transposes(2)
        h_out(2, 0, S_COPY)
        cw_regroup(S_COPY, 2, CW_SPLIT, E)
        h_out(2, 1, S_COPY)
        centroid_rows(1)
        z_out(0, 0)
        z_out(0, 1)
        cw_quantise(0)
        cw_regroup(V_COPY, 2, 0, CW_SPLIT)
        cw_quantise(1)
        z_quantise(0)
        cw_quantise(2)
        stage1(1, 0)
        stage1(1, 1)
        transposes(3)
        rows_mm(0, 0, 0)
        h_quantise(2)
        h_out(3, 0, S_COPY)
        h_out(3, 1, S_COPY)

        for i in range(N_UNITS - 1):
            if ok(i + 5):
                load_h(i + 5)
            if i == N_UNITS - 5:
                nc.sync.dma_start(out=cent_last[:], in_=centroids[CD:CD + 1, :].rearrange("o d -> (o d)").partition_broadcast(P))
            rows_mm(i, 0, 1)
            cols_mm(i, 0)
            z_out(i + 1, 0)
            rows_sub(i, 0, 0)
            if ok(i + 2):
                stage1(i + 2, 0)
            rows_mm(i, 1, 0)
            z_out(i + 1, 1)
            cols_square(i, 0)
            rows_square(i, 0, 0)
            rows_sub(i, 0, 1)
            rows_square(i, 0, 1)
            if ok(i + 4):
                transposes(i + 4)
            rows_mm(i, 1, 1)
            cols_mm(i, 1)
            if ok(i + 4):
                h_out(i + 4, 0, S_COPY)
            z_quantise(i + 1)
            if ok(i + 3):
                h_quantise(i + 3)
            if ok(i - 1):
                cols_add(i - 1, hcodes[i + 3] if ok(i + 3) else None)
            rows_sub(i, 1, 0)
            rows_sub(i, 1, 1)
            cols_square(i, 1)
            rows_square(i, 1, 0)
            if ok(i - 2):
                cols_reduce(i - 2)
            rows_mm(i + 1, 0, 0)
            if ok(i + 4):
                h_out(i + 4, 1, V_COPY if i % 4 == 2 else S_COPY)
            if ok(i + 2):
                stage1(i + 2, 1)
            rows_square(i, 1, 1)

        last = N_UNITS - 1
        for jl in range(UNIT):
            for c in range(C):
                if (jl, c) != (0, 0):
                    rows_mm(last, jl, c)
                rows_sub(last, jl, c)
                if (jl, c) == (1, 2):
                    cols_reduce(last - 2)
                    cols_reduce(last - 1)
                    rows_square_v(last, jl, c)
                else:
                    rows_square(last, jl, c)
                if (jl, c) == (0, 0):
                    cols_add(last - 1, None)

        nc.vector.tensor_copy(out=dist[:, CD, 0:last * UNIT], in_=dist_ps[:, 0:last * UNIT])

        dv = dist[:].rearrange("p c j -> p j c")
        neg = -1.0 / (2.0 * LS * LS)
        dmin = const.tile([P, J], F32)
        nc.vector.tensor_reduce(out=dmin[:], in_=dv, axis=AX.X, op=ALU.min)
        kv = const.tile([P, J, C], F32)
        nc.scalar.activation(out=kv[:], in_=dv, func=ACT.Exp, scale=neg)
        nc.sync.dma_start(out=out_2.rearrange("(p j) c -> p j c", j=J), in_=kv[:])
        shifted = const.tile([P, J, C], F32)
        nc.vector.tensor_tensor(out=shifted[:], in0=dv, in1=dmin[:].unsqueeze(2).to_broadcast([P, J, C]), op=ALU.subtract)
        ex = const.tile([P, J, C], F32)
        nc.scalar.activation(out=ex[:], in_=shifted[:], func=ACT.Exp, scale=neg)
        kmax = const.tile([P, J], F32)
        nc.vector.tensor_reduce(out=kmax[:], in_=kv[:], axis=AX.X, op=ALU.max)
        unc = const.tile([P, J], F32)
        nc.vector.tensor_scalar(out=unc[:], in0=kmax[:], scalar1=-1.0, scalar2=1.0, op0=ALU.mult, op1=ALU.add)
        nc.sync.dma_start(out=out_3.rearrange("(p j) -> p j", j=J), in_=unc[:])
        ssum = const.tile([P, J], F32)
        nc.vector.tensor_reduce(out=ssum[:], in_=ex[:], axis=AX.X, op=ALU.add)
        rsum = const.tile([P, J], F32)
        nc.vector.reciprocal(out=rsum[:], in_=ssum[:])
        probs = const.tile([P, J, C], F32)
        nc.vector.tensor_tensor(out=probs[:], in0=ex[:], in1=rsum[:].unsqueeze(2).to_broadcast([P, J, C]), op=ALU.mult)
        nc.sync.dma_start(out=out_0.rearrange("(p j) c -> p j c", j=J), in_=probs[:])
        nc.scalar.dma_start(out=out_1.rearrange("o (p j) c -> (o p) j c", j=J), in_=probs[:])
